import numpy as np
import ml_dtypes


def mxq(x, axis, fmt="e4m3"):
    dtype, down = {"e4m3": (ml_dtypes.float8_e4m3fn, 7), "e5m2": (ml_dtypes.float8_e5m2, 14)}[fmt]
    v = np.moveaxis(np.asarray(x, np.float32).astype(ml_dtypes.bfloat16).astype(np.float64), axis, -1)
    blocks = v.reshape(v.shape[:-1] + (-1, 32))
    amax = np.abs(blocks).max(-1, keepdims=True)
    byte = np.maximum(np.where(amax > 0, np.frexp(amax)[1] - 1 + 127, 0) - down, 1)
    scale = np.exp2(byte - 127.0)
    codes = (blocks / scale).astype(np.float32).astype(dtype).astype(np.float64)
    return np.moveaxis((codes * scale).reshape(v.shape), -1, axis)


WIDE = False


def mx_kscale(k):
    if not WIDE:
        return np.ones(k)
    levels = np.array([10, -10, 5, -5, 0])
    a = np.random.permutation(np.resize(levels, k // 512 * 4)).reshape(k // 512, 4)
    idx = np.arange(k)
    return np.exp2(a[idx // 512, idx % 128 // 32])


BF16 = ml_dtypes.bfloat16


def bf(x):
    return np.asarray(x, np.float32).astype(BF16)


def f64(x):
    return np.asarray(x).astype(np.float64)


N, C_IN, C_OUT, C_DGRAM, C_AA, C_ESM = 64, 512, 1024, 39, 22, 1280
LN_EPS = 1e-5


def layer_norm(x, g, b):
    mu = x.mean(-1, keepdims=True)
    var = x.var(-1, keepdims=True)
    return (x - mu) * (1.0 / np.sqrt(var + LN_EPS)) * g + b


def setup_inputs():
    rn, ru = np.random.standard_normal, np.random.uniform
    s = mx_kscale(C_IN)

    def vec():
        return bf(rn(C_OUT) * 0.1)

    def row():
        return bf(rn(C_OUT)[None, :])

    return {
        "act_dgram": bf(rn((N, N, C_OUT)) * 0.2),
        "aa_proj1": bf(rn((N, C_OUT)) * 0.6),
        "aa_proj2": bf(rn((N, C_OUT)) * 0.6),
        "esm_proj1": bf(rn((N, C_OUT))),
        "esm_proj2": bf(rn((N, C_OUT))),
        "query_embedding": bf(rn((N, N, C_IN)) * (0.5 + 1.5 * ru(size=(N, N)))[..., None] + rn((N, N))[..., None]),
        "pseudo_beta_mask": bf(ru(size=N)),
        "backbone_mask": bf(ru(size=N)),
        "multichain_mask_2d": bf(ru(size=(N, N))),
        "unit_x": bf(rn((N, N))),
        "unit_y": bf(rn((N, N))),
        "unit_z": bf(rn((N, N))),
        "ln_g": bf((1.0 + 0.1 * rn(C_IN)) * s),
        "ln_b": bf(0.1 * rn(C_IN) * s),
        "w_q": bf(rn((C_IN, C_OUT)) / np.sqrt(C_IN) / s[:, None]),
        "b_q": vec(),
        "w_pbm": row(), "b_pbm": vec(),
        "w_x": row(), "b_x": vec(),
        "w_y": row(), "b_y": vec(),
        "w_z": row(), "b_z": vec(),
        "w_bb": row(), "b_bb": vec(),
    }


def reference(act_dgram, aa_proj1, aa_proj2, esm_proj1, esm_proj2, query_embedding,
              pseudo_beta_mask, backbone_mask, multichain_mask_2d, unit_x, unit_y, unit_z,
              ln_g, ln_b, w_q, b_q, w_pbm, b_pbm, w_x, b_x, w_y, b_y, w_z, b_z, w_bb, b_bb):
    pbm, bbm, mc = f64(pseudo_beta_mask), f64(backbone_mask), f64(multichain_mask_2d)
    pb2 = pbm[:, None] * pbm[None, :] * mc
    bb2 = bbm[:, None] * bbm[None, :] * mc
    act = f64(act_dgram)
    act = act + (pb2[..., None] * f64(w_pbm)[0] + f64(b_pbm))
    act = act + f64(aa_proj1)[None, :, :]
    act = act + f64(aa_proj2)[:, None, :]
    act = act + ((f64(unit_x) * bb2)[..., None] * f64(w_x)[0] + f64(b_x))
    act = act + ((f64(unit_y) * bb2)[..., None] * f64(w_y)[0] + f64(b_y))
    act = act + ((f64(unit_z) * bb2)[..., None] * f64(w_z)[0] + f64(b_z))
    act = act + (bb2[..., None] * f64(w_bb)[0] + f64(b_bb))
    act = act + f64(esm_proj1)[None, :, :]
    act = act + f64(esm_proj2)[:, None, :]
    q = layer_norm(f64(query_embedding), f64(ln_g), f64(ln_b))
    act = act + (mxq(q, 2, "e4m3") @ mxq(f64(w_q), 0, "e4m3")) + f64(b_q)
    return act

@@ -1,0 +1,429 @@
+from contextlib import ExitStack
+
+import concourse.mybir as mybir
+from concourse.masks import make_identity
+
+F32 = mybir.dt.float32
+BF16 = mybir.dt.bfloat16
+U32 = mybir.dt.uint32
+U8 = mybir.dt.uint8
+FP8X4 = mybir.dt.float8_e4m3fn_x4
+ALU = mybir.AluOpType
+ACT = mybir.ActivationFunctionType
+
+P = 128
+N_RES = 64
+C_IN = 512
+C_OUT = 1024
+PACK = 4
+TILES = N_RES * N_RES // P
+BANK = 512
+BANKS = C_OUT // BANK
+LN_EPS = 1e-5
+
+PLAIN_COLS = 384
+VEC_COLS = C_OUT - PLAIN_COLS
+VEC_CHUNKS = VEC_COLS // P
+
+K_J = 0
+K_I = 64
+K_W = 96
+K_ONE = 101
+K_END = 107
+N_W = K_ONE - K_W
+I_HALF = N_RES // 2
+
+X_AHEAD = 4
+ACT_AHEAD = 2
+
+FLOPS = 2 * N_RES * N_RES * C_IN * C_OUT
+
+
+def tile_templatepairembeddermultimer_pa_t_kernel(
+    tc,
+    act_dgram,
+    aa_proj1,
+    aa_proj2,
+    esm_proj1,
+    esm_proj2,
+    query_embedding,
+    pseudo_beta_mask,
+    backbone_mask,
+    multichain_mask_2d,
+    unit_x,
+    unit_y,
+    unit_z,
+    ln_g,
+    ln_b,
+    w_q,
+    b_q,
+    w_pbm,
+    b_pbm,
+    w_x,
+    b_x,
+    w_y,
+    b_y,
+    w_z,
+    b_z,
+    w_bb,
+    b_bb,
+    out,
+):
+    nc = tc.nc
+    x_rows = query_embedding.flatten_outer_dims()
+    act_rows = act_dgram.flatten_outer_dims()
+    out_rows = out.flatten_outer_dims()
+    rank_one_rows = (w_x, w_y, w_z, w_bb, w_pbm)
+    bias_rows = (b_q, b_pbm, b_x, b_y, b_z, b_bb)
+
+    with ExitStack() as stack:
+        stack.enter_context(tc.manual_schedule())
+        const = stack.enter_context(tc.tile_pool(name="const", bufs=1))
+        setup = stack.enter_context(tc.tile_pool(name="setup", bufs=1))
+        x_pool = stack.enter_context(tc.tile_pool(name="x", bufs=X_AHEAD + 2))
+        act_pool = stack.enter_context(tc.tile_pool(name="act", bufs=ACT_AHEAD + 2))
+        stat_pool = stack.enter_context(tc.tile_pool(name="stat", bufs=4))
+        work = stack.enter_context(tc.tile_pool(name="work", bufs=2))
+        res_pool = stack.enter_context(tc.tile_pool(name="res", bufs=3))
+        psum_two = stack.enter_context(tc.psum_pool(name="psum_two", bufs=2))
+        psum_one = stack.enter_context(tc.psum_pool(name="psum_one", bufs=1))
+
+        x_tiles = {}
+        act_tiles = {}
+
+        def load_x(t):
+            x_tile = x_pool.tile([P, C_IN], BF16)
+            nc.sync.dma_start(out=x_tile[:], in_=x_rows[t * P : (t + 1) * P, :])
+            x_tiles[t] = x_tile
+
+        def load_act(t):
+            act_tile = act_pool.tile([P, C_OUT], BF16)
+            nc.sync.dma_start(out=act_tile[:], in_=act_rows[t * P : (t + 1) * P, :])
+            act_tiles[t] = act_tile
+
+        ident = const.tile([P, P], F32)
+        make_identity(nc, ident[:])
+        ident_bf = const.tile([P, P], BF16)
+        make_identity(nc, ident_bf[:])
+        neg_half = const.tile([P, 1], F32)
+        nc.vector.memset(neg_half[:], -0.5)
+
+        for t in range(X_AHEAD):
+            load_x(t)
+
+        vec_rows = setup.tile([P, P], BF16)
+        nc.vector.memset(vec_rows[:], 0.0)
+        nc.sync.dma_start(out=vec_rows[0:PACK, :], in_=ln_g.rearrange("(u p) -> u p", p=P))
+        nc.sync.dma_start(out=vec_rows[PACK : 2 * PACK, :], in_=ln_b.rearrange("(u p) -> u p", p=P))
+        residue_masks = (backbone_mask, pseudo_beta_mask)
+        for m in range(2):
+            nc.sync.dma_start(
+                out=vec_rows[2 * PACK + m : 2 * PACK + m + 1, :].rearrange("o (h j) -> o h j", h=2),
+                in_=residue_masks[m].unsqueeze(0).unsqueeze(0).to_broadcast([1, 2, N_RES]),
+            )
+        pair_rows = setup.tile([P, P], BF16)
+        pair_inputs = (multichain_mask_2d, unit_x, unit_y, unit_z)
+        for x in range(4):
+            nc.sync.dma_start(
+                out=pair_rows[x * TILES : (x + 1) * TILES, :],
+                in_=pair_inputs[x].rearrange("(t h) j -> t (h j)", h=2),
+            )
+        mask_rows = setup.tile([P, 2, N_RES], BF16)
+        for m in range(2):
+            nc.sync.dma_start(out=mask_rows[:, m, :], in_=residue_masks[m].partition_broadcast(P))
+
+        table_a = setup.tile([P, 2, C_OUT], BF16)
+        table_e = setup.tile([P, 2, C_OUT], BF16)
+        nc.vector.memset(table_a[K_W:P, :, :], 0.0)
+        nc.vector.memset(table_e[K_W:P, :, :], 0.0)
+        nc.sync.dma_start(
+            out=table_a[K_J : K_J + N_RES, :, :], in_=aa_proj1.unsqueeze(1).to_broadcast([N_RES, 2, C_OUT])
+        )
+        nc.sync.dma_start(
+            out=table_e[K_J : K_J + N_RES, :, :], in_=esm_proj1.unsqueeze(1).to_broadcast([N_RES, 2, C_OUT])
+        )
+        nc.sync.dma_start(out=table_a[K_I : K_I + I_HALF, :, :], in_=aa_proj2.rearrange("(s m) c -> m s c", s=2))
+        nc.sync.dma_start(out=table_e[K_I : K_I + I_HALF, :, :], in_=esm_proj2.rearrange("(s m) c -> m s c", s=2))
+        for f in range(N_W):
+            nc.sync.dma_start(
+                out=table_a[K_W + f : K_W + f + 1, :, :],
+                in_=rank_one_rows[f].unsqueeze(1).to_broadcast([1, 2, C_OUT]),
+            )
+        for b in range(len(bias_rows)):
+            nc.sync.dma_start(
+                out=table_a[K_ONE + b : K_ONE + b + 1, :, :],
+                in_=bias_rows[b].unsqueeze(0).unsqueeze(0).to_broadcast([1, 2, C_OUT]),
+            )
+
+        w_raw = setup.tile([P, PACK, C_OUT], BF16)
+        nc.sync.dma_start(out=w_raw[:], in_=w_q.rearrange("(u p) c -> p u c", p=P))
+
+        w_all = const.tile([P, N_W, VEC_COLS], BF16)
+        for f in range(N_W):
+            nc.sync.dma_start(
+                out=w_all[:, f, :],
+                in_=rank_one_rows[f].rearrange("o c -> (o c)")[PLAIN_COLS:C_OUT].partition_broadcast(P),
+            )
+
+        for t in range(ACT_AHEAD):
+            load_act(t)
+
+        feat = const.tile([P, TILES, P], F32)
+        nc.vector.memset(feat[:, :, K_I:P], 0.0)
+        nc.vector.memset(feat[:, :, K_ONE:K_END], 1.0)
+        one_hot_j = setup.tile([P, N_RES], F32)
+        nc.vector.tensor_tensor(out=one_hot_j[:], in0=ident[:, 0:N_RES], in1=ident[:, N_RES:P], op=ALU.add)
+        nc.vector.tensor_copy(
+            out=feat[:, :, K_J : K_J + N_RES], in_=one_hot_j[:].unsqueeze(1).to_broadcast([P, TILES, N_RES])
+        )
+        feat_halves = feat[:].rearrange("p (s t) k -> p s (t k)", s=2)
+        diagonal_step = P + 2
+        for h in range(2):
+            first = K_I + h
+            nc.vector.memset(
+                feat_halves[h * N_RES : (h + 1) * N_RES, :, first : first + (TILES // 2 - 1) * diagonal_step + 1 : diagonal_step],
+                1.0,
+            )
+
+        vec_cols_ps = psum_two.tile([P, P], BF16, tag="product")
+        nc.tensor.transpose(vec_cols_ps[:], vec_rows[:], ident_bf[:])
+        pair_cols_ps = psum_two.tile([P, P], BF16, tag="product")
+        nc.tensor.transpose(pair_cols_ps[:], pair_rows[:], ident_bf[:])
+        vec_cols = const.tile([P, 2 * PACK + 2], F32)
+        nc.vector.tensor_copy(out=vec_cols[:], in_=vec_cols_ps[:, 0 : 2 * PACK + 2])
+
+        pair_mask = setup.tile([P, 2, TILES], F32)
+        for h in range(2):
+            half = slice(h * N_RES, (h + 1) * N_RES)
+            for m in range(2):
+                nc.vector.tensor_scalar(
+                    out=pair_mask[half, m, :],
+                    in0=mask_rows[half, m, h:N_RES:2],
+                    scalar1=vec_cols[half, 2 * PACK + m : 2 * PACK + m + 1],
+                    scalar2=None,
+                    op0=ALU.mult,
+                )
+        nc.vector.tensor_tensor(
+            out=pair_mask[:],
+            in0=pair_mask[:],
+            in1=pair_cols_ps[:, 0:TILES].unsqueeze(1).to_broadcast([P, 2, TILES]),
+            op=ALU.mult,
+        )
+        nc.vector.tensor_tensor(
+            out=feat[:, :, K_W : K_W + 3].rearrange("p t x -> p x t"),
+            in0=pair_cols_ps[:, TILES:P].rearrange("p (x t) -> p x t", x=3),
+            in1=pair_mask[:, 0:1, :].to_broadcast([P, 3, TILES]),
+            op=ALU.mult,
+        )
+        nc.vector.tensor_copy(out=feat[:, :, K_W + 3 : K_W + 5].rearrange("p t m -> p m t"), in_=pair_mask[:])
+
+        table = const.tile([P, 2, C_OUT], F32)
+        nc.vector.tensor_tensor(out=table[:], in0=table_a[:], in1=table_e[:], op=ALU.add)
+
+        a_cols = const.tile([P, VEC_CHUNKS, N_RES], F32)
+        b_cols = const.tile([P, VEC_CHUNKS, N_RES], F32)
+        for c in range(VEC_CHUNKS):
+            chunk = slice(PLAIN_COLS + c * P, PLAIN_COLS + (c + 1) * P)
+            table_t = psum_two.tile([P, 2, P], F32, tag="product")
+            for s in range(2):
+                nc.tensor.transpose(table_t[:, s, :], table[:, s, chunk], ident[:])
+            nc.vector.tensor_copy(out=a_cols[:, c, :], in_=table_t[:, 0, K_J : K_J + N_RES])
+            bias_sum = stat_pool.tile([P, 1], F32)
+            nc.vector.reduce_sum(out=bias_sum[:], in_=table_t[:, 0, K_ONE:K_END], axis=mybir.AxisListType.X)
+            nc.vector.tensor_scalar(
+                out=b_cols[:, c, :].rearrange("p (s m) -> p s m", s=2),
+                in0=table_t[:, :, K_I : K_I + I_HALF],
+                scalar1=bias_sum[:, 0:1],
+                scalar2=None,
+                op0=ALU.add,
+            )
+
+        w_grouped = setup.tile([P, C_OUT, PACK], BF16, align_bytes=64)
+        nc.vector.tensor_copy(
+            out=w_grouped[:].rearrange("p (c i) u -> p c u i", i=4),
+            in_=w_raw[:].rearrange("p u (c i) -> p c u i", i=4),
+        )
+        w_codes = const.tile([P, C_OUT], U32, align_bytes=64)
+        w_scales = const.tile([P, C_OUT], U8, align_bytes=64)
+        nc.vector.quantize_mx(
+            out=w_codes[:].bitcast(FP8X4), scales=w_scales[:], in_=w_grouped[:].rearrange("p c u -> p (c u)")
+        )
+
+        moments = {}
+        x_hats = {}
+        x_hat_ts = {}
+        q_ts = {}
+        q_words = {}
+        products = {}
+        feat_t_banks = {}
+        feat_ts = {}
+        ab_ts = {}
+        extras = {}
+        results = {}
+
+        def ln_sum(t):
+            unread_sum = work.tile([P, C_IN], BF16)
+            row_sum = stat_pool.tile([P, 1], F32)
+            nc.scalar.activation(out=unread_sum[:], in_=x_tiles[t][:], func=ACT.Identity, accum_out=row_sum[:])
+            moment = stat_pool.tile([P, 4], F32)
+            nc.gpsimd.tensor_scalar(
+                out=moment[:, 0:1], in0=row_sum[:], scalar1=-1.0 / C_IN, scalar2=0.0, op0=ALU.mult, op1=ALU.add
+            )
+            moments[t] = moment
+
+        def ln_var(t):
+            moment = moments[t]
+            unread_sq = work.tile([P, C_IN], BF16)
+            sq_sum = stat_pool.tile([P, 1], F32)
+            nc.scalar.activation(
+                out=unread_sq[:], in_=x_tiles[t][:], func=ACT.Square, bias=moment[:, 0:1], accum_out=sq_sum[:]
+            )
+            nc.gpsimd.tensor_scalar(
+                out=moment[:, 1:2], in0=sq_sum[:], scalar1=1.0 / C_IN, scalar2=LN_EPS, op0=ALU.mult, op1=ALU.add
+            )
+            nc.gpsimd.tensor_tensor(out=moment[:, 2:3], in0=moment[:, 1:2], in1=neg_half[:], op=ALU.pow)
+            nc.gpsimd.tensor_tensor(out=moment[:, 3:4], in0=moment[:, 0:1], in1=moment[:, 2:3], op=ALU.mult)
+
+        def ln_norm(t):
+            moment = moments[t]
+            x_hat = work.tile([P, C_IN], F32)
+            nc.scalar.activation(
+                out=x_hat[:], in_=x_tiles[t][:], func=ACT.Identity, scale=moment[:, 2:3], bias=moment[:, 3:4]
+            )
+            x_hats[t] = x_hat
+
+        def ln_transpose(t):
+            x_hat_t = psum_one.tile([P, PACK, P], F32)
+            for u in range(PACK):
+                nc.tensor.transpose(x_hat_t[:, u, :], x_hats[t][:, u * P : (u + 1) * P], ident[:])
+            x_hat_ts[t] = x_hat_t
+
+        def ln_affine(t):
+            q_t = work.tile([P, P, PACK], BF16, align_bytes=64)
+            for u in range(PACK):
+                nc.scalar.activation(
+                    out=q_t[:, :, u],
+                    in_=x_hat_ts[t][:, u, :],
+                    func=ACT.Identity,
+                    scale=vec_cols[:, u : u + 1],
+                    bias=vec_cols[:, PACK + u : PACK + u + 1],
+                )
+            q_ts[t] = q_t
+
+        def quantise(t):
+            q_codes = work.tile([P, P], U32, align_bytes=64)
+            q_scales = work.tile([P, P], U8, align_bytes=64)
+            nc.vector.quantize_mx(
+                out=q_codes[:].bitcast(FP8X4), scales=q_scales[:], in_=q_ts[t][:].rearrange("p r u -> p (r u)")
+            )
+            q_words[t] = (q_codes, q_scales)
+
+        def project(t):
+            q_codes, q_scales = q_words[t]
+            product = psum_two.tile([P, C_OUT], F32)
+            for bank in range(BANKS):
+                cols = slice(bank * BANK, (bank + 1) * BANK)
+                nc.tensor.matmul_mx(
+                    out=product[:, cols],
+                    lhsT=q_codes[:].bitcast(FP8X4),
+                    lhsT_scale=q_scales[:],
+                    rhs=w_codes[:, cols].bitcast(FP8X4),
+                    rhs_scale=w_scales[:, cols],
+                    start=True,
+                    stop=True,
+                )
+            products[t] = product
+
+        def feat_transpose(t):
+            feat_t_ps = psum_one.tile([P, P], F32)
+            nc.tensor.transpose(feat_t_ps[:], feat[:, t, :], ident[:])
+            feat_t_banks[t] = feat_t_ps
+
+        def feat_copy(t):
+            feat_t = work.tile([P, P], F32)
+            nc.scalar.copy(out=feat_t[:], in_=feat_t_banks[t][:])
+            feat_ts[t] = feat_t
+
+        def ab_build(t):
+            ab_t = work.tile([P, VEC_CHUNKS, P], F32)
+            for c in range(VEC_CHUNKS):
+                for h in range(2):
+                    i = 2 * t + h
+                    nc.scalar.activation(
+                        out=ab_t[:, c, h * N_RES : (h + 1) * N_RES],
+                        in_=a_cols[:, c, :],
+                        func=ACT.Identity,
+                        bias=b_cols[:, c, i : i + 1],
+                    )
+            ab_ts[t] = ab_t
+
+        def small_terms(t):
+            extra = psum_one.tile([P, C_OUT], F32)
+            for c in range(VEC_CHUNKS):
+                chunk = slice(PLAIN_COLS + c * P, PLAIN_COLS + (c + 1) * P)
+                nc.tensor.transpose(extra[:, chunk], ab_ts[t][:, c, :], ident[:])
+            nc.tensor.matmul(
+                out=extra[:, 0:PLAIN_COLS],
+                lhsT=feat_ts[t][:],
+                rhs=table[:, t // (TILES // 2), 0:PLAIN_COLS],
+                start=True,
+                stop=True,
+            )
+            extras[t] = extra
+
+        def combine_start(t):
+            result = res_pool.tile([P, C_OUT], F32)
+            for bank in reversed(range(BANKS)):
+                cols = slice(bank * BANK, (bank + 1) * BANK)
+                nc.vector.tensor_tensor(
+                    out=result[:, cols], in0=act_tiles[t][:, cols], in1=extras[t][:, cols], op=ALU.add
+                )
+            results[t] = result
+
+        def combine_rank_one(t):
+            result = results[t]
+            for f in range(N_W):
+                for bank in reversed(range(BANKS)):
+                    lo = max(PLAIN_COLS, bank * BANK)
+                    hi = (bank + 1) * BANK
+                    nc.vector.scalar_tensor_tensor(
+                        out=result[:, lo:hi],
+                        in0=w_all[:, f, lo - PLAIN_COLS : hi - PLAIN_COLS],
+                        scalar=feat[:, t, K_W + f : K_W + f + 1],
+                        in1=result[:, lo:hi],
+                        op0=ALU.mult,
+                        op1=ALU.add,
+                    )
+
+        def combine_finish(t):
+            result = results[t]
+            for bank in reversed(range(BANKS)):
+                cols = slice(bank * BANK, (bank + 1) * BANK)
+                nc.vector.tensor_tensor(out=result[:, cols], in0=result[:, cols], in1=products[t][:, cols], op=ALU.add)
+
+        def store(t):
+            nc.sync.dma_start(out=out_rows[t * P : (t + 1) * P, :], in_=results[t][:])
+
+        def each(stage, t):
+            if 0 <= t < TILES:
+                stage(t)
+
+        for n in range(-3, TILES + 1):
+            if n >= 0:
+                each(load_x, n + X_AHEAD)
+                each(load_act, n + ACT_AHEAD)
+            each(store, n - 1)
+            each(ln_norm, n + 1)
+            each(ln_transpose, n + 1)
+            each(feat_transpose, n + 2)
+            each(ln_sum, n + 3)
+            each(ln_var, n + 2)
+            each(ab_build, n + 1)
+            each(feat_copy, n + 2)
+            each(ln_affine, n + 1)
+            each(combine_start, n)
+            each(small_terms, n + 1)
+            each(combine_rank_one, n)
+            each(quantise, n + 1)
+            each(project, n + 1)
+            each(combine_finish, n)

@@ -260,6 +260,7 @@ def tile_templatepairembeddermultimer_pa_t_kernel(
         ab_ts = {}
         extras = {}
         results = {}
+        partials = {}
 
         def ln_sum(t):
             unread_sum = work.tile([P, C_IN], BF16)
@@ -371,35 +372,47 @@ def tile_templatepairembeddermultimer_pa_t_kernel(
             )
             extras[t] = extra
 
-        def combine_start(t):
+        def combine_open(t):
             result = res_pool.tile([P, C_OUT], F32)
+            partial = work.tile([P, VEC_COLS], F32)
             for bank in reversed(range(BANKS)):
                 cols = slice(bank * BANK, (bank + 1) * BANK)
                 nc.vector.tensor_tensor(
                     out=result[:, cols], in0=act_tiles[t][:, cols], in1=extras[t][:, cols], op=ALU.add
                 )
+            for bank in reversed(range(BANKS)):
+                lo = max(PLAIN_COLS, bank * BANK)
+                hi = (bank + 1) * BANK
+                nc.vector.scalar_tensor_tensor(
+                    out=partial[:, lo - PLAIN_COLS : hi - PLAIN_COLS],
+                    in0=w_all[:, 0, lo - PLAIN_COLS : hi - PLAIN_COLS],
+                    scalar=feat[:, t, K_W : K_W + 1],
+                    in1=products[t][:, lo:hi],
+                    op0=ALU.mult,
+                    op1=ALU.add,
+                )
+            nc.vector.tensor_tensor(
+                out=result[:, 0:PLAIN_COLS], in0=result[:, 0:PLAIN_COLS], in1=products[t][:, 0:PLAIN_COLS], op=ALU.add
+            )
             results[t] = result
+            partials[t] = partial
 
         def combine_rank_one(t):
-            result = results[t]
-            for f in range(N_W):
-                for bank in reversed(range(BANKS)):
-                    lo = max(PLAIN_COLS, bank * BANK)
-                    hi = (bank + 1) * BANK
-                    nc.vector.scalar_tensor_tensor(
-                        out=result[:, lo:hi],
-                        in0=w_all[:, f, lo - PLAIN_COLS : hi - PLAIN_COLS],
-                        scalar=feat[:, t, K_W + f : K_W + f + 1],
-                        in1=result[:, lo:hi],
-                        op0=ALU.mult,
-                        op1=ALU.add,
-                    )
+            for f in range(1, N_W):
+                running = results[t][:, PLAIN_COLS:C_OUT] if f % 2 == 1 else partials[t][:]
+                nc.vector.scalar_tensor_tensor(
+                    out=running,
+                    in0=w_all[:, f, :],
+                    scalar=feat[:, t, K_W + f : K_W + f + 1],
+                    in1=running,
+                    op0=ALU.mult,
+                    op1=ALU.add,
+                )
 
-        def combine_finish(t):
-            result = results[t]
-            for bank in reversed(range(BANKS)):
-                cols = slice(bank * BANK, (bank + 1) * BANK)
-                nc.vector.tensor_tensor(out=result[:, cols], in0=result[:, cols], in1=products[t][:, cols], op=ALU.add)
+        def combine_close(t):
+            nc.gpsimd.tensor_tensor(
+                out=results[t][:, PLAIN_COLS:C_OUT], in0=results[t][:, PLAIN_COLS:C_OUT], in1=partials[t][:], op=ALU.add
+            )
 
         def store(t):
             nc.sync.dma_start(out=out_rows[t * P : (t + 1) * P, :], in_=results[t][:])
@@ -412,6 +425,7 @@ def tile_templatepairembeddermultimer_pa_t_kernel(
             if n >= 0:
                 each(load_x, n + X_AHEAD)
                 each(load_act, n + ACT_AHEAD)
+            each(combine_close, n - 1)
             each(store, n - 1)
             each(ln_norm, n + 1)
             each(ln_transpose, n + 1)
@@ -421,9 +435,8 @@ def tile_templatepairembeddermultimer_pa_t_kernel(
             each(ab_build, n + 1)
             each(feat_copy, n + 2)
             each(ln_affine, n + 1)
-            each(combine_start, n)
+            each(combine_open, n)
             each(small_terms, n + 1)
             each(combine_rank_one, n)
             each(quantise, n + 1)
             each(project, n + 1)
-            each(combine_finish, n)

@@ -33,7 +33,10 @@ K_END = 107
 N_W = K_ONE - K_W
 I_HALF = N_RES // 2
 
-X_AHEAD = 4
+SUMMED_TERMS = 2
+CHAINED_TERMS = N_W - SUMMED_TERMS
+
+X_AHEAD = 6
 ACT_AHEAD = 2
 
 FLOPS = 2 * N_RES * N_RES * C_IN * C_OUT
@@ -82,7 +85,7 @@ def tile_templatepairembeddermultimer_pa_t_kernel(
         setup = stack.enter_context(tc.tile_pool(name="setup", bufs=1))
         x_pool = stack.enter_context(tc.tile_pool(name="x", bufs=X_AHEAD + 2))
         act_pool = stack.enter_context(tc.tile_pool(name="act", bufs=ACT_AHEAD + 2))
-        stat_pool = stack.enter_context(tc.tile_pool(name="stat", bufs=4))
+        stat_pool = stack.enter_context(tc.tile_pool(name="stat", bufs=6))
         work = stack.enter_context(tc.tile_pool(name="work", bufs=2))
         res_pool = stack.enter_context(tc.tile_pool(name="res", bufs=3))
         psum_two = stack.enter_context(tc.psum_pool(name="psum_two", bufs=2))
@@ -158,8 +161,8 @@ def tile_templatepairembeddermultimer_pa_t_kernel(
         w_raw = setup.tile([P, PACK, C_OUT], BF16)
         nc.sync.dma_start(out=w_raw[:], in_=w_q.rearrange("(u p) c -> p u c", p=P))
 
-        w_all = const.tile([P, N_W, VEC_COLS], BF16)
-        for f in range(N_W):
+        w_all = const.tile([P, CHAINED_TERMS, VEC_COLS], BF16)
+        for f in range(CHAINED_TERMS):
             nc.sync.dma_start(
                 out=w_all[:, f, :],
                 in_=rank_one_rows[f].rearrange("o c -> (o c)")[PLAIN_COLS:C_OUT].partition_broadcast(P),
@@ -220,14 +223,19 @@ def tile_templatepairembeddermultimer_pa_t_kernel(
         table = const.tile([P, 2, C_OUT], F32)
         nc.vector.tensor_tensor(out=table[:], in0=table_a[:], in1=table_e[:], op=ALU.add)
 
-        a_cols = const.tile([P, VEC_CHUNKS, N_RES], F32)
+        a_twice = const.tile([P, VEC_CHUNKS, 2, N_RES], F32)
         b_cols = const.tile([P, VEC_CHUNKS, N_RES], F32)
+        w_cols = const.tile([P, VEC_CHUNKS, N_W], F32)
         for c in range(VEC_CHUNKS):
             chunk = slice(PLAIN_COLS + c * P, PLAIN_COLS + (c + 1) * P)
             table_t = psum_two.tile([P, 2, P], F32, tag="product")
             for s in range(2):
                 nc.tensor.transpose(table_t[:, s, :], table[:, s, chunk], ident[:])
-            nc.vector.tensor_copy(out=a_cols[:, c, :], in_=table_t[:, 0, K_J : K_J + N_RES])
+            nc.vector.tensor_copy(
+                out=a_twice[:, c, :, :],
+                in_=table_t[:, 0, K_J : K_J + N_RES].unsqueeze(1).to_broadcast([P, 2, N_RES]),
+            )
+            nc.vector.tensor_copy(out=w_cols[:, c, :], in_=table_t[:, 0, K_W : K_W + N_W])
             bias_sum = stat_pool.tile([P, 1], F32)
             nc.vector.reduce_sum(out=bias_sum[:], in_=table_t[:, 0, K_ONE:K_END], axis=mybir.AxisListType.X)
             nc.vector.tensor_scalar(
@@ -255,9 +263,9 @@ def tile_templatepairembeddermultimer_pa_t_kernel(
         q_ts = {}
         q_words = {}
         products = {}
-        feat_t_banks = {}
+        sides = {}
         feat_ts = {}
-        ab_ts = {}
+        summands = {}
         extras = {}
         results = {}
         partials = {}
@@ -336,33 +344,60 @@ def tile_templatepairembeddermultimer_pa_t_kernel(
             products[t] = product
 
         def feat_transpose(t):
-            feat_t_ps = psum_one.tile([P, P], F32)
-            nc.tensor.transpose(feat_t_ps[:], feat[:, t, :], ident[:])
-            feat_t_banks[t] = feat_t_ps
+            side = psum_one.tile([P, 1 + SUMMED_TERMS, P], F32)
+            nc.tensor.transpose(side[:, 0, :], feat[:, t, :], ident[:])
+            for s in range(SUMMED_TERMS):
+                k = K_W + CHAINED_TERMS + s
+                nc.tensor.transpose(side[:, 1 + s, :], feat[:, t, k : k + 1].to_broadcast([P, P]), ident[:])
+            sides[t] = side
 
         def feat_copy(t):
             feat_t = work.tile([P, P], F32)
-            nc.scalar.copy(out=feat_t[:], in_=feat_t_banks[t][:])
+            nc.scalar.copy(out=feat_t[:], in_=sides[t][:, 0, :])
             feat_ts[t] = feat_t
 
-        def ab_build(t):
-            ab_t = work.tile([P, VEC_CHUNKS, P], F32)
+        def multiply(t):
+            summand = work.tile([P, SUMMED_TERMS, VEC_CHUNKS, P], F32)
             for c in range(VEC_CHUNKS):
                 for h in range(2):
                     i = 2 * t + h
                     nc.scalar.activation(
-                        out=ab_t[:, c, h * N_RES : (h + 1) * N_RES],
-                        in_=a_cols[:, c, :],
+                        out=summand[:, 0, c, h * N_RES : (h + 1) * N_RES],
+                        in_=sides[t][:, 1, h * N_RES : (h + 1) * N_RES],
                         func=ACT.Identity,
+                        scale=w_cols[:, c, CHAINED_TERMS : CHAINED_TERMS + 1],
                         bias=b_cols[:, c, i : i + 1],
                     )
-            ab_ts[t] = ab_t
+                for s in range(1, SUMMED_TERMS):
+                    nc.scalar.activation(
+                        out=summand[:, s, c, :],
+                        in_=sides[t][:, 1 + s, :],
+                        func=ACT.Identity,
+                        scale=w_cols[:, c, CHAINED_TERMS + s : CHAINED_TERMS + s + 1],
+                    )
+            summands[t] = summand
 
         def small_terms(t):
             extra = psum_one.tile([P, C_OUT], F32)
-            for c in range(VEC_CHUNKS):
+            for c in reversed(range(VEC_CHUNKS)):
                 chunk = slice(PLAIN_COLS + c * P, PLAIN_COLS + (c + 1) * P)
-                nc.tensor.transpose(extra[:, chunk], ab_ts[t][:, c, :], ident[:])
+                nc.tensor.matmul(
+                    out=extra[:, chunk],
+                    lhsT=a_twice[:, c, :, :].rearrange("p h j -> p (h j)"),
+                    rhs=ident[:],
+                    is_transpose=True,
+                    start=True,
+                    stop=False,
+                )
+                for s in range(SUMMED_TERMS):
+                    nc.tensor.matmul(
+                        out=extra[:, chunk],
+                        lhsT=summands[t][:, s, c, :],
+                        rhs=ident[:],
+                        is_transpose=True,
+                        start=False,
+                        stop=(s == SUMMED_TERMS - 1),
+                    )
             nc.tensor.matmul(
                 out=extra[:, 0:PLAIN_COLS],
                 lhsT=feat_ts[t][:],
@@ -398,7 +433,7 @@ def tile_templatepairembeddermultimer_pa_t_kernel(
             partials[t] = partial
 
         def combine_rank_one(t):
-            for f in range(1, N_W):
+            for f in range(1, CHAINED_TERMS):
                 running = results[t][:, PLAIN_COLS:C_OUT] if f % 2 == 1 else partials[t][:]
                 nc.vector.scalar_tensor_tensor(
                     out=running,
@@ -421,22 +456,22 @@ def tile_templatepairembeddermultimer_pa_t_kernel(
             if 0 <= t < TILES:
                 stage(t)
 
-        for n in range(-3, TILES + 1):
+        for n in range(-5, TILES + 1):
             if n >= 0:
                 each(load_x, n + X_AHEAD)
                 each(load_act, n + ACT_AHEAD)
             each(combine_close, n - 1)
             each(store, n - 1)
-            each(ln_norm, n + 1)
-            each(ln_transpose, n + 1)
-            each(feat_transpose, n + 2)
-            each(ln_sum, n + 3)
-            each(ln_var, n + 2)
-            each(ab_build, n + 1)
+            each(ln_affine, n + 2)
+            each(ln_norm, n + 3)
             each(feat_copy, n + 2)
-            each(ln_affine, n + 1)
+            each(multiply, n + 2)
+            each(ln_var, n + 4)
+            each(ln_sum, n + 5)
+            each(project, n + 1)
             each(combine_open, n)
             each(small_terms, n + 1)
+            each(ln_transpose, n + 3)
+            each(feat_transpose, n + 3)
             each(combine_rank_one, n)
-            each(quantise, n + 1)
-            each(project, n + 1)
+            each(quantise, n + 2)

@@ -36,7 +36,10 @@ I_HALF = N_RES // 2
 SUMMED_TERMS = 2
 CHAINED_TERMS = N_W - SUMMED_TERMS
 
-X_AHEAD = 6
+PLAIN_PIECES = 2
+PIECE_COLS = PLAIN_COLS // PLAIN_PIECES
+
+X_AHEAD = 7
 ACT_AHEAD = 2
 
 FLOPS = 2 * N_RES * N_RES * C_IN * C_OUT
@@ -188,9 +191,9 @@ def tile_templatepairembeddermultimer_pa_t_kernel(
                 1.0,
             )
 
-        vec_cols_ps = psum_two.tile([P, P], BF16, tag="product")
+        vec_cols_ps = psum_two.tile([P, P], BF16, tag="extra")
         nc.tensor.transpose(vec_cols_ps[:], vec_rows[:], ident_bf[:])
-        pair_cols_ps = psum_two.tile([P, P], BF16, tag="product")
+        pair_cols_ps = psum_two.tile([P, P], BF16, tag="extra")
         nc.tensor.transpose(pair_cols_ps[:], pair_rows[:], ident_bf[:])
         vec_cols = const.tile([P, 2 * PACK + 2], F32)
         nc.vector.tensor_copy(out=vec_cols[:], in_=vec_cols_ps[:, 0 : 2 * PACK + 2])
@@ -228,7 +231,7 @@ def tile_templatepairembeddermultimer_pa_t_kernel(
         w_cols = const.tile([P, VEC_CHUNKS, N_W], F32)
         for c in range(VEC_CHUNKS):
             chunk = slice(PLAIN_COLS + c * P, PLAIN_COLS + (c + 1) * P)
-            table_t = psum_two.tile([P, 2, P], F32, tag="product")
+            table_t = psum_two.tile([P, 2, P], F32, tag="extra")
             for s in range(2):
                 nc.tensor.transpose(table_t[:, s, :], table[:, s, chunk], ident[:])
             nc.vector.tensor_copy(
@@ -260,7 +263,8 @@ def tile_templatepairembeddermultimer_pa_t_kernel(
         moments = {}
         x_hats = {}
         x_hat_ts = {}
-        q_ts = {}
+        q_planes = {}
+        q_groupeds = {}
         q_words = {}
         products = {}
         sides = {}
@@ -308,28 +312,38 @@ def tile_templatepairembeddermultimer_pa_t_kernel(
             x_hat_ts[t] = x_hat_t
 
         def ln_affine(t):
-            q_t = work.tile([P, P, PACK], BF16, align_bytes=64)
+            q_plane = work.tile([P, PACK, P], BF16)
             for u in range(PACK):
                 nc.scalar.activation(
-                    out=q_t[:, :, u],
+                    out=q_plane[:, u, :],
                     in_=x_hat_ts[t][:, u, :],
                     func=ACT.Identity,
                     scale=vec_cols[:, u : u + 1],
                     bias=vec_cols[:, PACK + u : PACK + u + 1],
                 )
-            q_ts[t] = q_t
+            q_planes[t] = q_plane
+
+        def regroup(t):
+            q_grouped = work.tile([P, P, PACK], BF16, align_bytes=64)
+            nc.vector.tensor_copy(
+                out=q_grouped[:].rearrange("p (r i) u -> p r u i", i=4),
+                in_=q_planes[t][:].rearrange("p u (r i) -> p r u i", i=4),
+            )
+            q_groupeds[t] = q_grouped
 
         def quantise(t):
             q_codes = work.tile([P, P], U32, align_bytes=64)
             q_scales = work.tile([P, P], U8, align_bytes=64)
             nc.vector.quantize_mx(
-                out=q_codes[:].bitcast(FP8X4), scales=q_scales[:], in_=q_ts[t][:].rearrange("p r u -> p (r u)")
+                out=q_codes[:].bitcast(FP8X4),
+                scales=q_scales[:],
+                in_=q_groupeds[t][:].rearrange("p r u -> p (r u)"),
             )
             q_words[t] = (q_codes, q_scales)
 
         def project(t):
             q_codes, q_scales = q_words[t]
-            product = psum_two.tile([P, C_OUT], F32)
+            product = psum_one.tile([P, C_OUT], F32)
             for bank in range(BANKS):
                 cols = slice(bank * BANK, (bank + 1) * BANK)
                 nc.tensor.matmul_mx(
@@ -377,12 +391,11 @@ def tile_templatepairembeddermultimer_pa_t_kernel(
                     )
             summands[t] = summand
 
-        def small_terms(t):
-            extra = psum_one.tile([P, C_OUT], F32)
-            for c in reversed(range(VEC_CHUNKS)):
+        def sum_chunks(t, chunks):
+            for c in chunks:
                 chunk = slice(PLAIN_COLS + c * P, PLAIN_COLS + (c + 1) * P)
                 nc.tensor.matmul(
-                    out=extra[:, chunk],
+                    out=extras[t][:, chunk],
                     lhsT=a_twice[:, c, :, :].rearrange("p h j -> p (h j)"),
                     rhs=ident[:],
                     is_transpose=True,
@@ -391,43 +404,61 @@ def tile_templatepairembeddermultimer_pa_t_kernel(
                 )
                 for s in range(SUMMED_TERMS):
                     nc.tensor.matmul(
-                        out=extra[:, chunk],
+                        out=extras[t][:, chunk],
                         lhsT=summands[t][:, s, c, :],
                         rhs=ident[:],
                         is_transpose=True,
                         start=False,
                         stop=(s == SUMMED_TERMS - 1),
                     )
+
+        def plain_piece(t, piece):
+            cols = slice(piece * PIECE_COLS, (piece + 1) * PIECE_COLS)
             nc.tensor.matmul(
-                out=extra[:, 0:PLAIN_COLS],
+                out=extras[t][:, cols],
                 lhsT=feat_ts[t][:],
-                rhs=table[:, t // (TILES // 2), 0:PLAIN_COLS],
+                rhs=table[:, t // (TILES // 2), cols],
                 start=True,
                 stop=True,
             )
+
+        def small_terms_first(t):
+            extra = psum_two.tile([P, C_OUT], F32)
             extras[t] = extra
+            sum_chunks(t, (4, 3))
+            plain_piece(t, 0)
+
+        def small_terms_second(t):
+            sum_chunks(t, (2,))
+
+        def small_terms_third(t):
+            sum_chunks(t, (1, 0))
+            plain_piece(t, 1)
 
         def combine_open(t):
             result = res_pool.tile([P, C_OUT], F32)
             partial = work.tile([P, VEC_COLS], F32)
-            for bank in reversed(range(BANKS)):
-                cols = slice(bank * BANK, (bank + 1) * BANK)
-                nc.vector.tensor_tensor(
-                    out=result[:, cols], in0=act_tiles[t][:, cols], in1=extras[t][:, cols], op=ALU.add
-                )
-            for bank in reversed(range(BANKS)):
-                lo = max(PLAIN_COLS, bank * BANK)
-                hi = (bank + 1) * BANK
-                nc.vector.scalar_tensor_tensor(
-                    out=partial[:, lo - PLAIN_COLS : hi - PLAIN_COLS],
-                    in0=w_all[:, 0, lo - PLAIN_COLS : hi - PLAIN_COLS],
-                    scalar=feat[:, t, K_W : K_W + 1],
-                    in1=products[t][:, lo:hi],
-                    op0=ALU.mult,
-                    op1=ALU.add,
-                )
+            first, second = slice(0, BANK), slice(BANK, C_OUT)
+            nc.vector.scalar_tensor_tensor(
+                out=partial[:, BANK - PLAIN_COLS : VEC_COLS],
+                in0=w_all[:, 0, BANK - PLAIN_COLS : VEC_COLS],
+                scalar=feat[:, t, K_W : K_W + 1],
+                in1=products[t][:, second],
+                op0=ALU.mult,
+                op1=ALU.add,
+            )
+            nc.vector.tensor_tensor(out=result[:, first], in0=act_tiles[t][:, first], in1=products[t][:, first], op=ALU.add)
+            nc.vector.tensor_tensor(out=result[:, second], in0=act_tiles[t][:, second], in1=extras[t][:, second], op=ALU.add)
+            nc.vector.scalar_tensor_tensor(
+                out=partial[:, 0 : BANK - PLAIN_COLS],
+                in0=w_all[:, 0, 0 : BANK - PLAIN_COLS],
+                scalar=feat[:, t, K_W : K_W + 1],
+                in1=extras[t][:, PLAIN_COLS:BANK],
+                op0=ALU.mult,
+                op1=ALU.add,
+            )
             nc.vector.tensor_tensor(
-                out=result[:, 0:PLAIN_COLS], in0=result[:, 0:PLAIN_COLS], in1=products[t][:, 0:PLAIN_COLS], op=ALU.add
+                out=result[:, 0:PLAIN_COLS], in0=result[:, 0:PLAIN_COLS], in1=extras[t][:, 0:PLAIN_COLS], op=ALU.add
             )
             results[t] = result
             partials[t] = partial
@@ -456,22 +487,25 @@ def tile_templatepairembeddermultimer_pa_t_kernel(
             if 0 <= t < TILES:
                 stage(t)
 
-        for n in range(-5, TILES + 1):
+        for n in range(-6, TILES + 1):
             if n >= 0:
                 each(load_x, n + X_AHEAD)
                 each(load_act, n + ACT_AHEAD)
             each(combine_close, n - 1)
             each(store, n - 1)
             each(ln_affine, n + 2)
-            each(ln_norm, n + 3)
             each(feat_copy, n + 2)
             each(multiply, n + 2)
-            each(ln_var, n + 4)
-            each(ln_sum, n + 5)
-            each(project, n + 1)
+            each(ln_norm, n + 4)
+            each(ln_var, n + 5)
+            each(ln_sum, n + 6)
             each(combine_open, n)
-            each(small_terms, n + 1)
+            each(small_terms_first, n + 1)
             each(ln_transpose, n + 3)
+            each(small_terms_second, n + 1)
+            each(project, n + 1)
+            each(small_terms_third, n + 1)
             each(feat_transpose, n + 3)
+            each(regroup, n + 2)
             each(combine_rank_one, n)
             each(quantise, n + 2)

@@ -260,6 +260,7 @@ def tile_templatepairembeddermultimer_pa_t_kernel(
             out=w_codes[:].bitcast(FP8X4), scales=w_scales[:], in_=w_grouped[:].rearrange("p c u -> p (c u)")
         )
 
+        neg_means = {}
         moments = {}
         x_hats = {}
         x_hat_ts = {}
@@ -276,32 +277,35 @@ def tile_templatepairembeddermultimer_pa_t_kernel(
 
         def ln_sum(t):
             unread_sum = work.tile([P, C_IN], BF16)
-            row_sum = stat_pool.tile([P, 1], F32)
-            nc.scalar.activation(out=unread_sum[:], in_=x_tiles[t][:], func=ACT.Identity, accum_out=row_sum[:])
-            moment = stat_pool.tile([P, 4], F32)
-            nc.gpsimd.tensor_scalar(
-                out=moment[:, 0:1], in0=row_sum[:], scalar1=-1.0 / C_IN, scalar2=0.0, op0=ALU.mult, op1=ALU.add
+            neg_mean = stat_pool.tile([P, 1], F32)
+            nc.scalar.activation(
+                out=unread_sum[:], in_=x_tiles[t][:], func=ACT.Identity, scale=-1.0 / C_IN, accum_out=neg_mean[:]
             )
-            moments[t] = moment
+            neg_means[t] = neg_mean
 
         def ln_var(t):
-            moment = moments[t]
             unread_sq = work.tile([P, C_IN], BF16)
             sq_sum = stat_pool.tile([P, 1], F32)
             nc.scalar.activation(
-                out=unread_sq[:], in_=x_tiles[t][:], func=ACT.Square, bias=moment[:, 0:1], accum_out=sq_sum[:]
+                out=unread_sq[:], in_=x_tiles[t][:], func=ACT.Square, bias=neg_means[t][:], accum_out=sq_sum[:]
             )
+            moment = stat_pool.tile([P, 3], F32)
             nc.gpsimd.tensor_scalar(
-                out=moment[:, 1:2], in0=sq_sum[:], scalar1=1.0 / C_IN, scalar2=LN_EPS, op0=ALU.mult, op1=ALU.add
+                out=moment[:, 0:1], in0=sq_sum[:], scalar1=1.0 / C_IN, scalar2=LN_EPS, op0=ALU.mult, op1=ALU.add
             )
-            nc.gpsimd.tensor_tensor(out=moment[:, 2:3], in0=moment[:, 1:2], in1=neg_half[:], op=ALU.pow)
-            nc.gpsimd.tensor_tensor(out=moment[:, 3:4], in0=moment[:, 0:1], in1=moment[:, 2:3], op=ALU.mult)
+            nc.gpsimd.tensor_tensor(out=moment[:, 1:2], in0=moment[:, 0:1], in1=neg_half[:], op=ALU.pow)
+            nc.gpsimd.tensor_tensor(out=moment[:, 2:3], in0=neg_means[t][:], in1=moment[:, 1:2], op=ALU.mult)
+            moments[t] = moment
 
         def ln_norm(t):
-            moment = moments[t]
             x_hat = work.tile([P, C_IN], F32)
-            nc.scalar.activation(
-                out=x_hat[:], in_=x_tiles[t][:], func=ACT.Identity, scale=moment[:, 2:3], bias=moment[:, 3:4]
+            nc.gpsimd.tensor_scalar(
+                out=x_hat[:],
+                in0=x_tiles[t][:],
+                scalar1=moments[t][:, 1:2],
+                scalar2=moments[t][:, 2:3],
+                op0=ALU.mult,
+                op1=ALU.add,
             )
             x_hats[t] = x_hat
 
@@ -493,12 +497,12 @@ def tile_templatepairembeddermultimer_pa_t_kernel(
                 each(load_act, n + ACT_AHEAD)
             each(combine_close, n - 1)
             each(store, n - 1)
-            each(ln_affine, n + 2)
-            each(feat_copy, n + 2)
-            each(multiply, n + 2)
             each(ln_norm, n + 4)
+            each(ln_affine, n + 2)
             each(ln_var, n + 5)
             each(ln_sum, n + 6)
+            each(feat_copy, n + 2)
+            each(multiply, n + 2)
             each(combine_open, n)
             each(small_terms_first, n + 1)
             each(ln_transpose, n + 3)

@@ -260,7 +260,6 @@ def tile_templatepairembeddermultimer_pa_t_kernel(
             out=w_codes[:].bitcast(FP8X4), scales=w_scales[:], in_=w_grouped[:].rearrange("p c u -> p (c u)")
         )
 
-        neg_means = {}
         moments = {}
         x_hats = {}
         x_hat_ts = {}
@@ -277,35 +276,32 @@ def tile_templatepairembeddermultimer_pa_t_kernel(
 
         def ln_sum(t):
             unread_sum = work.tile([P, C_IN], BF16)
-            neg_mean = stat_pool.tile([P, 1], F32)
-            nc.scalar.activation(
-                out=unread_sum[:], in_=x_tiles[t][:], func=ACT.Identity, scale=-1.0 / C_IN, accum_out=neg_mean[:]
+            row_sum = stat_pool.tile([P, 1], F32)
+            nc.scalar.activation(out=unread_sum[:], in_=x_tiles[t][:], func=ACT.Identity, accum_out=row_sum[:])
+            moment = stat_pool.tile([P, 4], F32)
+            nc.gpsimd.tensor_scalar(
+                out=moment[:, 0:1], in0=row_sum[:], scalar1=-1.0 / C_IN, scalar2=0.0, op0=ALU.mult, op1=ALU.add
             )
-            neg_means[t] = neg_mean
+            moments[t] = moment
 
         def ln_var(t):
+            moment = moments[t]
             unread_sq = work.tile([P, C_IN], BF16)
             sq_sum = stat_pool.tile([P, 1], F32)
             nc.scalar.activation(
-                out=unread_sq[:], in_=x_tiles[t][:], func=ACT.Square, bias=neg_means[t][:], accum_out=sq_sum[:]
+                out=unread_sq[:], in_=x_tiles[t][:], func=ACT.Square, bias=moment[:, 0:1], accum_out=sq_sum[:]
             )
-            moment = stat_pool.tile([P, 3], F32)
             nc.gpsimd.tensor_scalar(
-                out=moment[:, 0:1], in0=sq_sum[:], scalar1=1.0 / C_IN, scalar2=LN_EPS, op0=ALU.mult, op1=ALU.add
+                out=moment[:, 1:2], in0=sq_sum[:], scalar1=1.0 / C_IN, scalar2=LN_EPS, op0=ALU.mult, op1=ALU.add
             )
-            nc.gpsimd.tensor_tensor(out=moment[:, 1:2], in0=moment[:, 0:1], in1=neg_half[:], op=ALU.pow)
-            nc.gpsimd.tensor_tensor(out=moment[:, 2:3], in0=neg_means[t][:], in1=moment[:, 1:2], op=ALU.mult)
-            moments[t] = moment
+            nc.gpsimd.tensor_tensor(out=moment[:, 2:3], in0=moment[:, 1:2], in1=neg_half[:], op=ALU.pow)
+            nc.gpsimd.tensor_tensor(out=moment[:, 3:4], in0=moment[:, 0:1], in1=moment[:, 2:3], op=ALU.mult)
 
         def ln_norm(t):
+            moment = moments[t]
             x_hat = work.tile([P, C_IN], F32)
-            nc.gpsimd.tensor_scalar(
-                out=x_hat[:],
-                in0=x_tiles[t][:],
-                scalar1=moments[t][:, 1:2],
-                scalar2=moments[t][:, 2:3],
-                op0=ALU.mult,
-                op1=ALU.add,
+            nc.scalar.activation(
+                out=x_hat[:], in_=x_tiles[t][:], func=ACT.Identity, scale=moment[:, 2:3], bias=moment[:, 3:4]
             )
             x_hats[t] = x_hat
 
@@ -480,7 +476,7 @@ def tile_templatepairembeddermultimer_pa_t_kernel(
                 )
 
         def combine_close(t):
-            nc.gpsimd.tensor_tensor(
+            nc.vector.tensor_tensor(
                 out=results[t][:, PLAIN_COLS:C_OUT], in0=results[t][:, PLAIN_COLS:C_OUT], in1=partials[t][:], op=ALU.add
             )
 
@@ -491,18 +487,16 @@ def tile_templatepairembeddermultimer_pa_t_kernel(
             if 0 <= t < TILES:
                 stage(t)
 
-        for n in range(-6, TILES + 1):
+        for n in range(-6, TILES):
             if n >= 0:
                 each(load_x, n + X_AHEAD)
                 each(load_act, n + ACT_AHEAD)
-            each(combine_close, n - 1)
-            each(store, n - 1)
-            each(ln_norm, n + 4)
             each(ln_affine, n + 2)
-            each(ln_var, n + 5)
-            each(ln_sum, n + 6)
             each(feat_copy, n + 2)
             each(multiply, n + 2)
+            each(ln_norm, n + 4)
+            each(ln_var, n + 5)
+            each(ln_sum, n + 6)
             each(combine_open, n)
             each(small_terms_first, n + 1)
             each(ln_transpose, n + 3)
@@ -513,3 +507,5 @@ def tile_templatepairembeddermultimer_pa_t_kernel(
             each(regroup, n + 2)
             each(combine_rank_one, n)
             each(quantise, n + 2)
+            each(combine_close, n)
+            each(store, n)

from contextlib import ExitStack

import concourse.mybir as mybir
from concourse.masks import make_identity

F32 = mybir.dt.float32
BF16 = mybir.dt.bfloat16
U32 = mybir.dt.uint32
U8 = mybir.dt.uint8
FP8X4 = mybir.dt.float8_e4m3fn_x4
ALU = mybir.AluOpType
ACT = mybir.ActivationFunctionType

P = 128
N_RES = 64
C_IN = 512
C_OUT = 1024
PACK = 4
TILES = N_RES * N_RES // P
BANK = 512
BANKS = C_OUT // BANK
LN_EPS = 1e-5

PLAIN_COLS = 384
VEC_COLS = C_OUT - PLAIN_COLS
VEC_CHUNKS = VEC_COLS // P

K_J = 0
K_I = 64
K_W = 96
K_ONE = 101
K_END = 107
N_W = K_ONE - K_W
I_HALF = N_RES // 2

SUMMED_TERMS = 2
CHAINED_TERMS = N_W - SUMMED_TERMS

PLAIN_PIECES = 2
PIECE_COLS = PLAIN_COLS // PLAIN_PIECES

X_AHEAD = 7
ACT_AHEAD = 2

FLOPS = 2 * N_RES * N_RES * C_IN * C_OUT


def tile_templatepairembeddermultimer_pa_t_kernel(
    tc,
    act_dgram,
    aa_proj1,
    aa_proj2,
    esm_proj1,
    esm_proj2,
    query_embedding,
    pseudo_beta_mask,
    backbone_mask,
    multichain_mask_2d,
    unit_x,
    unit_y,
    unit_z,
    ln_g,
    ln_b,
    w_q,
    b_q,
    w_pbm,
    b_pbm,
    w_x,
    b_x,
    w_y,
    b_y,
    w_z,
    b_z,
    w_bb,
    b_bb,
    out,
):
    nc = tc.nc
    x_rows = query_embedding.flatten_outer_dims()
    act_rows = act_dgram.flatten_outer_dims()
    out_rows = out.flatten_outer_dims()
    rank_one_rows = (w_x, w_y, w_z, w_bb, w_pbm)
    bias_rows = (b_q, b_pbm, b_x, b_y, b_z, b_bb)

    with ExitStack() as stack:
        stack.enter_context(tc.manual_schedule())
        const = stack.enter_context(tc.tile_pool(name="const", bufs=1))
        setup = stack.enter_context(tc.tile_pool(name="setup", bufs=1))
        x_pool = stack.enter_context(tc.tile_pool(name="x", bufs=X_AHEAD + 2))
        act_pool = stack.enter_context(tc.tile_pool(name="act", bufs=ACT_AHEAD + 2))
        stat_pool = stack.enter_context(tc.tile_pool(name="stat", bufs=6))
        work = stack.enter_context(tc.tile_pool(name="work", bufs=2))
        res_pool = stack.enter_context(tc.tile_pool(name="res", bufs=3))
        psum_two = stack.enter_context(tc.psum_pool(name="psum_two", bufs=2))
        psum_one = stack.enter_context(tc.psum_pool(name="psum_one", bufs=1))

        x_tiles = {}
        act_tiles = {}

        def load_x(t):
            x_tile = x_pool.tile([P, C_IN], BF16)
            nc.sync.dma_start(out=x_tile[:], in_=x_rows[t * P : (t + 1) * P, :])
            x_tiles[t] = x_tile

        def load_act(t):
            act_tile = act_pool.tile([P, C_OUT], BF16)
            nc.sync.dma_start(out=act_tile[:], in_=act_rows[t * P : (t + 1) * P, :])
            act_tiles[t] = act_tile

        ident = const.tile([P, P], F32)
        make_identity(nc, ident[:])
        ident_bf = const.tile([P, P], BF16)
        make_identity(nc, ident_bf[:])
        neg_half = const.tile([P, 1], F32)
        nc.vector.memset(neg_half[:], -0.5)

        for t in range(X_AHEAD):
            load_x(t)

        vec_rows = setup.tile([P, P], BF16)
        nc.vector.memset(vec_rows[:], 0.0)
        nc.sync.dma_start(out=vec_rows[0:PACK, :], in_=ln_g.rearrange("(u p) -> u p", p=P))
        nc.sync.dma_start(out=vec_rows[PACK : 2 * PACK, :], in_=ln_b.rearrange("(u p) -> u p", p=P))
        residue_masks = (backbone_mask, pseudo_beta_mask)
        for m in range(2):
            nc.sync.dma_start(
                out=vec_rows[2 * PACK + m : 2 * PACK + m + 1, :].rearrange("o (h j) -> o h j", h=2),
                in_=residue_masks[m].unsqueeze(0).unsqueeze(0).to_broadcast([1, 2, N_RES]),
            )
        pair_rows = setup.tile([P, P], BF16)
        pair_inputs = (multichain_mask_2d, unit_x, unit_y, unit_z)
        for x in range(4):
            nc.sync.dma_start(
                out=pair_rows[x * TILES : (x + 1) * TILES, :],
                in_=pair_inputs[x].rearrange("(t h) j -> t (h j)", h=2),
            )
        mask_rows = setup.tile([P, 2, N_RES], BF16)
        for m in range(2):
            nc.sync.dma_start(out=mask_rows[:, m, :], in_=residue_masks[m].partition_broadcast(P))

        table_a = setup.tile([P, 2, C_OUT], BF16)
        table_e = setup.tile([P, 2, C_OUT], BF16)
        nc.vector.memset(table_a[K_W:P, :, :], 0.0)
        nc.vector.memset(table_e[K_W:P, :, :], 0.0)
        nc.sync.dma_start(
            out=table_a[K_J : K_J + N_RES, :, :], in_=aa_proj1.unsqueeze(1).to_broadcast([N_RES, 2, C_OUT])
        )
        nc.sync.dma_start(
            out=table_e[K_J : K_J + N_RES, :, :], in_=esm_proj1.unsqueeze(1).to_broadcast([N_RES, 2, C_OUT])
        )
        nc.sync.dma_start(out=table_a[K_I : K_I + I_HALF, :, :], in_=aa_proj2.rearrange("(s m) c -> m s c", s=2))
        nc.sync.dma_start(out=table_e[K_I : K_I + I_HALF, :, :], in_=esm_proj2.rearrange("(s m) c -> m s c", s=2))
        for f in range(N_W):
            nc.sync.dma_start(
                out=table_a[K_W + f : K_W + f + 1, :, :],
                in_=rank_one_rows[f].unsqueeze(1).to_broadcast([1, 2, C_OUT]),
            )
        for b in range(len(bias_rows)):
            nc.sync.dma_start(
                out=table_a[K_ONE + b : K_ONE + b + 1, :, :],
                in_=bias_rows[b].unsqueeze(0).unsqueeze(0).to_broadcast([1, 2, C_OUT]),
            )

        w_raw = setup.tile([P, PACK, C_OUT], BF16)
        nc.sync.dma_start(out=w_raw[:], in_=w_q.rearrange("(u p) c -> p u c", p=P))

        w_all = const.tile([P, CHAINED_TERMS, VEC_COLS], BF16)
        for f in range(CHAINED_TERMS):
            nc.sync.dma_start(
                out=w_all[:, f, :],
                in_=rank_one_rows[f].rearrange("o c -> (o c)")[PLAIN_COLS:C_OUT].partition_broadcast(P),
            )

        for t in range(ACT_AHEAD):
            load_act(t)

        feat = const.tile([P, TILES, P], F32)
        nc.vector.memset(feat[:, :, K_I:P], 0.0)
        nc.vector.memset(feat[:, :, K_ONE:K_END], 1.0)
        one_hot_j = setup.tile([P, N_RES], F32)
        nc.vector.tensor_tensor(out=one_hot_j[:], in0=ident[:, 0:N_RES], in1=ident[:, N_RES:P], op=ALU.add)
        nc.vector.tensor_copy(
            out=feat[:, :, K_J : K_J + N_RES], in_=one_hot_j[:].unsqueeze(1).to_broadcast([P, TILES, N_RES])
        )
        feat_halves = feat[:].rearrange("p (s t) k -> p s (t k)", s=2)
        diagonal_step = P + 2
        for h in range(2):
            first = K_I + h
            nc.vector.memset(
                feat_halves[h * N_RES : (h + 1) * N_RES, :, first : first + (TILES // 2 - 1) * diagonal_step + 1 : diagonal_step],
                1.0,
            )

        vec_cols_ps = psum_two.tile([P, P], BF16, tag="extra")
        nc.tensor.transpose(vec_cols_ps[:], vec_rows[:], ident_bf[:])
        pair_cols_ps = psum_two.tile([P, P], BF16, tag="extra")
        nc.tensor.transpose(pair_cols_ps[:], pair_rows[:], ident_bf[:])
        vec_cols = const.tile([P, 2 * PACK + 2], F32)
        nc.vector.tensor_copy(out=vec_cols[:], in_=vec_cols_ps[:, 0 : 2 * PACK + 2])

        pair_mask = setup.tile([P, 2, TILES], F32)
        for h in range(2):
            half = slice(h * N_RES, (h + 1) * N_RES)
            for m in range(2):
                nc.vector.tensor_scalar(
                    out=pair_mask[half, m, :],
                    in0=mask_rows[half, m, h:N_RES:2],
                    scalar1=vec_cols[half, 2 * PACK + m : 2 * PACK + m + 1],
                    scalar2=None,
                    op0=ALU.mult,
                )
        nc.vector.tensor_tensor(
            out=pair_mask[:],
            in0=pair_mask[:],
            in1=pair_cols_ps[:, 0:TILES].unsqueeze(1).to_broadcast([P, 2, TILES]),
            op=ALU.mult,
        )
        nc.vector.tensor_tensor(
            out=feat[:, :, K_W : K_W + 3].rearrange("p t x -> p x t"),
            in0=pair_cols_ps[:, TILES:P].rearrange("p (x t) -> p x t", x=3),
            in1=pair_mask[:, 0:1, :].to_broadcast([P, 3, TILES]),
            op=ALU.mult,
        )
        nc.vector.tensor_copy(out=feat[:, :, K_W + 3 : K_W + 5].rearrange("p t m -> p m t"), in_=pair_mask[:])

        table = const.tile([P, 2, C_OUT], F32)
        nc.vector.tensor_tensor(out=table[:], in0=table_a[:], in1=table_e[:], op=ALU.add)

        a_twice = const.tile([P, VEC_CHUNKS, 2, N_RES], F32)
        b_cols = const.tile([P, VEC_CHUNKS, N_RES], F32)
        w_cols = const.tile([P, VEC_CHUNKS, N_W], F32)
        for c in range(VEC_CHUNKS):
            chunk = slice(PLAIN_COLS + c * P, PLAIN_COLS + (c + 1) * P)
            table_t = psum_two.tile([P, 2, P], F32, tag="extra")
            for s in range(2):
                nc.tensor.transpose(table_t[:, s, :], table[:, s, chunk], ident[:])
            nc.vector.tensor_copy(
                out=a_twice[:, c, :, :],
                in_=table_t[:, 0, K_J : K_J + N_RES].unsqueeze(1).to_broadcast([P, 2, N_RES]),
            )
            nc.vector.tensor_copy(out=w_cols[:, c, :], in_=table_t[:, 0, K_W : K_W + N_W])
            bias_sum = stat_pool.tile([P, 1], F32)
            nc.vector.reduce_sum(out=bias_sum[:], in_=table_t[:, 0, K_ONE:K_END], axis=mybir.AxisListType.X)
            nc.vector.tensor_scalar(
                out=b_cols[:, c, :].rearrange("p (s m) -> p s m", s=2),
                in0=table_t[:, :, K_I : K_I + I_HALF],
                scalar1=bias_sum[:, 0:1],
                scalar2=None,
                op0=ALU.add,
            )

        w_grouped = setup.tile([P, C_OUT, PACK], BF16, align_bytes=64)
        nc.vector.tensor_copy(
            out=w_grouped[:].rearrange("p (c i) u -> p c u i", i=4),
            in_=w_raw[:].rearrange("p u (c i) -> p c u i", i=4),
        )
        w_codes = const.tile([P, C_OUT], U32, align_bytes=64)
        w_scales = const.tile([P, C_OUT], U8, align_bytes=64)
        nc.vector.quantize_mx(
            out=w_codes[:].bitcast(FP8X4), scales=w_scales[:], in_=w_grouped[:].rearrange("p c u -> p (c u)")
        )

        moments = {}
        x_hats = {}
        x_hat_ts = {}
        q_planes = {}
        q_groupeds = {}
        q_words = {}
        products = {}
        sides = {}
        feat_ts = {}
        summands = {}
        extras = {}
        results = {}
        partials = {}

        def ln_sum(t):
            unread_sum = work.tile([P, C_IN], BF16)
            row_sum = stat_pool.tile([P, 1], F32)
            nc.scalar.activation(out=unread_sum[:], in_=x_tiles[t][:], func=ACT.Identity, accum_out=row_sum[:])
            moment = stat_pool.tile([P, 4], F32)
            nc.gpsimd.tensor_scalar(
                out=moment[:, 0:1], in0=row_sum[:], scalar1=-1.0 / C_IN, scalar2=0.0, op0=ALU.mult, op1=ALU.add
            )
            moments[t] = moment

        def ln_var(t):
            moment = moments[t]
            unread_sq = work.tile([P, C_IN], BF16)
            sq_sum = stat_pool.tile([P, 1], F32)
            nc.scalar.activation(
                out=unread_sq[:], in_=x_tiles[t][:], func=ACT.Square, bias=moment[:, 0:1], accum_out=sq_sum[:]
            )
            nc.gpsimd.tensor_scalar(
                out=moment[:, 1:2], in0=sq_sum[:], scalar1=1.0 / C_IN, scalar2=LN_EPS, op0=ALU.mult, op1=ALU.add
            )
            nc.gpsimd.tensor_tensor(out=moment[:, 2:3], in0=moment[:, 1:2], in1=neg_half[:], op=ALU.pow)
            nc.gpsimd.tensor_tensor(out=moment[:, 3:4], in0=moment[:, 0:1], in1=moment[:, 2:3], op=ALU.mult)

        def ln_norm(t):
            moment = moments[t]
            x_hat = work.tile([P, C_IN], F32)
            nc.scalar.activation(
                out=x_hat[:], in_=x_tiles[t][:], func=ACT.Identity, scale=moment[:, 2:3], bias=moment[:, 3:4]
            )
            x_hats[t] = x_hat

        def ln_transpose(t):
            x_hat_t = psum_one.tile([P, PACK, P], F32)
            for u in range(PACK):
                nc.tensor.transpose(x_hat_t[:, u, :], x_hats[t][:, u * P : (u + 1) * P], ident[:])
            x_hat_ts[t] = x_hat_t

        def ln_affine(t):
            q_plane = work.tile([P, PACK, P], BF16)
            for u in range(PACK):
                nc.scalar.activation(
                    out=q_plane[:, u, :],
                    in_=x_hat_ts[t][:, u, :],
                    func=ACT.Identity,
                    scale=vec_cols[:, u : u + 1],
                    bias=vec_cols[:, PACK + u : PACK + u + 1],
                )
            q_planes[t] = q_plane

        def regroup(t):
            q_grouped = work.tile([P, P, PACK], BF16, align_bytes=64)
            nc.vector.tensor_copy(
                out=q_grouped[:].rearrange("p (r i) u -> p r u i", i=4),
                in_=q_planes[t][:].rearrange("p u (r i) -> p r u i", i=4),
            )
            q_groupeds[t] = q_grouped

        def quantise(t):
            q_codes = work.tile([P, P], U32, align_bytes=64)
            q_scales = work.tile([P, P], U8, align_bytes=64)
            nc.vector.quantize_mx(
                out=q_codes[:].bitcast(FP8X4),
                scales=q_scales[:],
                in_=q_groupeds[t][:].rearrange("p r u -> p (r u)"),
            )
            q_words[t] = (q_codes, q_scales)

        def project(t):
            q_codes, q_scales = q_words[t]
            product = psum_one.tile([P, C_OUT], F32)
            for bank in range(BANKS):
                cols = slice(bank * BANK, (bank + 1) * BANK)
                nc.tensor.matmul_mx(
                    out=product[:, cols],
                    lhsT=q_codes[:].bitcast(FP8X4),
                    lhsT_scale=q_scales[:],
                    rhs=w_codes[:, cols].bitcast(FP8X4),
                    rhs_scale=w_scales[:, cols],
                    start=True,
                    stop=True,
                )
            products[t] = product

        def feat_transpose(t):
            side = psum_one.tile([P, 1 + SUMMED_TERMS, P], F32)
            nc.tensor.transpose(side[:, 0, :], feat[:, t, :], ident[:])
            for s in range(SUMMED_TERMS):
                k = K_W + CHAINED_TERMS + s
                nc.tensor.transpose(side[:, 1 + s, :], feat[:, t, k : k + 1].to_broadcast([P, P]), ident[:])
            sides[t] = side

        def feat_copy(t):
            feat_t = work.tile([P, P], F32)
            nc.scalar.copy(out=feat_t[:], in_=sides[t][:, 0, :])
            feat_ts[t] = feat_t

        def multiply(t):
            summand = work.tile([P, SUMMED_TERMS, VEC_CHUNKS, P], F32)
            for c in range(VEC_CHUNKS):
                for h in range(2):
                    i = 2 * t + h
                    nc.scalar.activation(
                        out=summand[:, 0, c, h * N_RES : (h + 1) * N_RES],
                        in_=sides[t][:, 1, h * N_RES : (h + 1) * N_RES],
                        func=ACT.Identity,
                        scale=w_cols[:, c, CHAINED_TERMS : CHAINED_TERMS + 1],
                        bias=b_cols[:, c, i : i + 1],
                    )
                for s in range(1, SUMMED_TERMS):
                    nc.scalar.activation(
                        out=summand[:, s, c, :],
                        in_=sides[t][:, 1 + s, :],
                        func=ACT.Identity,
                        scale=w_cols[:, c, CHAINED_TERMS + s : CHAINED_TERMS + s + 1],
                    )
            summands[t] = summand

        def sum_chunks(t, chunks):
            for c in chunks:
                chunk = slice(PLAIN_COLS + c * P, PLAIN_COLS + (c + 1) * P)
                nc.tensor.matmul(
                    out=extras[t][:, chunk],
                    lhsT=a_twice[:, c, :, :].rearrange("p h j -> p (h j)"),
                    rhs=ident[:],
                    is_transpose=True,
                    start=True,
                    stop=False,
                )
                for s in range(SUMMED_TERMS):
                    nc.tensor.matmul(
                        out=extras[t][:, chunk],
                        lhsT=summands[t][:, s, c, :],
                        rhs=ident[:],
                        is_transpose=True,
                        start=False,
                        stop=(s == SUMMED_TERMS - 1),
                    )

        def plain_piece(t, piece):
            cols = slice(piece * PIECE_COLS, (piece + 1) * PIECE_COLS)
            nc.tensor.matmul(
                out=extras[t][:, cols],
                lhsT=feat_ts[t][:],
                rhs=table[:, t // (TILES // 2), cols],
                start=True,
                stop=True,
            )

        def small_terms_first(t):
            extra = psum_two.tile([P, C_OUT], F32)
            extras[t] = extra
            sum_chunks(t, (4, 3))
            plain_piece(t, 0)

        def small_terms_second(t):
            sum_chunks(t, (2,))

        def small_terms_third(t):
            sum_chunks(t, (1, 0))
            plain_piece(t, 1)

        def combine_open(t):
            result = res_pool.tile([P, C_OUT], F32)
            partial = work.tile([P, VEC_COLS], F32)
            first, second = slice(0, BANK), slice(BANK, C_OUT)
            nc.vector.scalar_tensor_tensor(
                out=partial[:, BANK - PLAIN_COLS : VEC_COLS],
                in0=w_all[:, 0, BANK - PLAIN_COLS : VEC_COLS],
                scalar=feat[:, t, K_W : K_W + 1],
                in1=products[t][:, second],
                op0=ALU.mult,
                op1=ALU.add,
            )
            nc.vector.tensor_tensor(out=result[:, first], in0=act_tiles[t][:, first], in1=products[t][:, first], op=ALU.add)
            nc.vector.tensor_tensor(out=result[:, second], in0=act_tiles[t][:, second], in1=extras[t][:, second], op=ALU.add)
            nc.vector.scalar_tensor_tensor(
                out=partial[:, 0 : BANK - PLAIN_COLS],
                in0=w_all[:, 0, 0 : BANK - PLAIN_COLS],
                scalar=feat[:, t, K_W : K_W + 1],
                in1=extras[t][:, PLAIN_COLS:BANK],
                op0=ALU.mult,
                op1=ALU.add,
            )
            nc.vector.tensor_tensor(
                out=result[:, 0:PLAIN_COLS], in0=result[:, 0:PLAIN_COLS], in1=extras[t][:, 0:PLAIN_COLS], op=ALU.add
            )
            results[t] = result
            partials[t] = partial

        def combine_rank_one(t):
            for f in range(1, CHAINED_TERMS):
                running = results[t][:, PLAIN_COLS:C_OUT] if f % 2 == 1 else partials[t][:]
                nc.vector.scalar_tensor_tensor(
                    out=running,
                    in0=w_all[:, f, :],
                    scalar=feat[:, t, K_W + f : K_W + f + 1],
                    in1=running,
                    op0=ALU.mult,
                    op1=ALU.add,
                )

        def combine_close(t):
            nc.vector.tensor_tensor(
                out=results[t][:, PLAIN_COLS:C_OUT], in0=results[t][:, PLAIN_COLS:C_OUT], in1=partials[t][:], op=ALU.add
            )

        def store(t):
            nc.sync.dma_start(out=out_rows[t * P : (t + 1) * P, :], in_=results[t][:])

        def each(stage, t):
            if 0 <= t < TILES:
                stage(t)

        for n in range(-6, TILES):
            if n >= 0:
                each(load_x, n + X_AHEAD)
                each(load_act, n + ACT_AHEAD)
            each(ln_affine, n + 2)
            each(feat_copy, n + 2)
            each(multiply, n + 2)
            each(ln_norm, n + 4)
            each(ln_var, n + 5)
            each(ln_sum, n + 6)
            each(combine_open, n)
            each(small_terms_first, n + 1)
            each(ln_transpose, n + 3)
            each(small_terms_second, n + 1)
            each(project, n + 1)
            each(small_terms_third, n + 1)
            each(feat_transpose, n + 3)
            each(regroup, n + 2)
            each(combine_rank_one, n)
            each(quantise, n + 2)
            each(combine_close, n)
            each(store, n)
